import numpy as np
import ml_dtypes

BF16 = ml_dtypes.bfloat16


def bf(x):
    return np.asarray(x, np.float32).astype(BF16)


def f32(x):
    return np.asarray(x, np.float32)


def f64(x):
    return np.asarray(x).astype(np.float64)


def striped(idx):
    return np.tile(idx.reshape(-1, 16).T, (8, 1))


D, S, M, L, N = 128, 4096, 256, 128, 2048


def silu(v):
    return v / (1.0 + np.exp(-v))


def setup_inputs():
    return {"table": bf(np.random.standard_normal((D, S))), "pos": bf(0.5 * np.random.standard_normal((D, L))), "w": bf(np.random.standard_normal((D, M)) / np.sqrt(D)), "offs": striped(np.random.permutation(np.tile(np.arange(S), 2))[:N])}


def reference(table, pos, w, offs):
    idx = offs[:16].T.reshape(-1)
    place = np.arange(N) % L
    return silu(f64(w).T @ f64(table)[:, idx] + (f64(w).T @ f64(pos))[:, place])

@@ -1,0 +1,61 @@
+import concourse.mybir as mybir
+
+BF16, F32, U16 = mybir.dt.bfloat16, mybir.dt.float32, mybir.dt.uint16
+SILU = mybir.ActivationFunctionType.Silu
+
+P = 128
+ITEMS = 4096
+PLACES = 128
+HIDDEN = 256
+N = 2048
+PIECE = 512
+HALVES = HIDDEN // P
+PIECES = N // PIECE
+
+FLOPS = 2 * P * HIDDEN * (N + PLACES)
+
+
+def tile_denoisedsasrec_kernel(tc, table, pos, w, offs, out):
+    nc = tc.nc
+    with (
+        tc.tile_pool(name="held", bufs=1) as held,
+        tc.tile_pool(name="results", bufs=4) as results,
+        tc.psum_pool(name="psum", bufs=1) as psum,
+    ):
+        offsets = held.tile([P, N // 16], U16, name="offsets")
+        weights = held.tile([P, HIDDEN], BF16, name="weights")
+        places = held.tile([P, PLACES], BF16, name="places")
+        items = held.tile([P, ITEMS], BF16, name="items")
+        nc.sync.dma_start(offsets[:], offs)
+        nc.scalar.dma_start(weights[:], w)
+        nc.scalar.dma_start(places[:], pos)
+        nc.sync.dma_start(items[:], table)
+
+        blocks = [(piece, half) for piece in range(PIECES) for half in range(HALVES)]
+        banks = [psum.tile([P, PIECE], F32, name=f"bank{b}") for b in range(len(blocks))]
+
+        sequences = PIECE // PLACES
+        repeated_places = places[:].unsqueeze(1).to_broadcast([P, sequences, PLACES])
+        for bank, (piece, half) in zip(banks, blocks):
+            nc.tensor.matmul(
+                bank[:].rearrange("p (s l) -> p s l", s=sequences),
+                weights[:, half * P : (half + 1) * P],
+                repeated_places,
+                start=True,
+                stop=False,
+            )
+
+        for bank, (piece, half) in zip(banks, blocks):
+            piece_offsets = offsets[:, piece * (PIECE // 16) : (piece + 1) * (PIECE // 16)]
+            nc.tensor.matmul(
+                bank[:],
+                weights[:, half * P : (half + 1) * P],
+                items[:].indirect(piece_offsets),
+                start=False,
+                stop=True,
+            )
+            result = results.tile([P, PIECE], F32, name="result")
+            nc.scalar.activation(result[:], bank[:], SILU)
+            nc.sync.dma_start(
+                out[half * P : (half + 1) * P, piece * PIECE : (piece + 1) * PIECE], result[:]
+            )

@@ -26,9 +26,9 @@ def tile_denoisedsasrec_kernel(tc, table, pos, w, offs, out):
         weights = held.tile([P, HIDDEN], BF16, name="weights")
         places = held.tile([P, PLACES], BF16, name="places")
         items = held.tile([P, ITEMS], BF16, name="items")
-        nc.sync.dma_start(offsets[:], offs)
         nc.scalar.dma_start(weights[:], w)
-        nc.scalar.dma_start(places[:], pos)
+        nc.sync.dma_start(places[:], pos)
+        nc.sync.dma_start(offsets[:], offs)
         nc.sync.dma_start(items[:], table)
 
         blocks = [(piece, half) for piece in range(PIECES) for half in range(HALVES)]

@@ -2,6 +2,7 @@ import concourse.mybir as mybir
 
 BF16, F32, U16 = mybir.dt.bfloat16, mybir.dt.float32, mybir.dt.uint16
 SILU = mybir.ActivationFunctionType.Silu
+ADD = mybir.AluOpType.add
 
 P = 128
 ITEMS = 4096
@@ -19,8 +20,9 @@ def tile_denoisedsasrec_kernel(tc, table, pos, w, offs, out):
     nc = tc.nc
     with (
         tc.tile_pool(name="held", bufs=1) as held,
-        tc.tile_pool(name="results", bufs=4) as results,
-        tc.psum_pool(name="psum", bufs=1) as psum,
+        tc.tile_pool(name="blocks", bufs=4) as blocks,
+        tc.psum_pool(name="once", bufs=1) as once,
+        tc.psum_pool(name="banks", bufs=4) as banks,
     ):
         offsets = held.tile([P, N // 16], U16, name="offsets")
         weights = held.tile([P, HIDDEN], BF16, name="weights")
@@ -31,31 +33,38 @@ def tile_denoisedsasrec_kernel(tc, table, pos, w, offs, out):
         nc.sync.dma_start(offsets[:], offs)
         nc.sync.dma_start(items[:], table)
 
-        blocks = [(piece, half) for piece in range(PIECES) for half in range(HALVES)]
-        banks = [psum.tile([P, PIECE], F32, name=f"bank{b}") for b in range(len(blocks))]
-
-        sequences = PIECE // PLACES
-        repeated_places = places[:].unsqueeze(1).to_broadcast([P, sequences, PLACES])
-        for bank, (piece, half) in zip(banks, blocks):
+        projected_bank = once.tile([P, HALVES, PLACES], F32, name="projected_bank")
+        projected = held.tile([P, HALVES, PLACES], F32, name="projected")
+        for half in range(HALVES):
             nc.tensor.matmul(
-                bank[:].rearrange("p (s l) -> p s l", s=sequences),
+                projected_bank[:, half, :],
                 weights[:, half * P : (half + 1) * P],
-                repeated_places,
+                places[:],
                 start=True,
-                stop=False,
-            )
-
-        for bank, (piece, half) in zip(banks, blocks):
-            piece_offsets = offsets[:, piece * (PIECE // 16) : (piece + 1) * (PIECE // 16)]
-            nc.tensor.matmul(
-                bank[:],
-                weights[:, half * P : (half + 1) * P],
-                items[:].indirect(piece_offsets),
-                start=False,
                 stop=True,
             )
-            result = results.tile([P, PIECE], F32, name="result")
-            nc.scalar.activation(result[:], bank[:], SILU)
-            nc.sync.dma_start(
-                out[half * P : (half + 1) * P, piece * PIECE : (piece + 1) * PIECE], result[:]
-            )
+        nc.vector.tensor_copy(projected[:], projected_bank[:])
+
+        sequences = PIECE // PLACES
+        for piece in range(PIECES):
+            piece_offsets = offsets[:, piece * (PIECE // 16) : (piece + 1) * (PIECE // 16)]
+            for half in range(HALVES):
+                bank = banks.tile([P, PIECE], F32, name="bank")
+                nc.tensor.matmul(
+                    bank[:],
+                    weights[:, half * P : (half + 1) * P],
+                    items[:].indirect(piece_offsets),
+                    start=True,
+                    stop=True,
+                )
+                block = blocks.tile([P, PIECE], F32, name="block")
+                nc.vector.tensor_tensor(
+                    block[:].rearrange("p (s l) -> p s l", s=sequences),
+                    bank[:].rearrange("p (s l) -> p s l", s=sequences),
+                    projected[:, half : half + 1, :].to_broadcast([P, sequences, PLACES]),
+                    ADD,
+                )
+                nc.scalar.activation(block[:], block[:], SILU)
+                nc.sync.dma_start(
+                    out[half * P : (half + 1) * P, piece * PIECE : (piece + 1) * PIECE], block[:]
+                )

@@ -2,7 +2,6 @@ import concourse.mybir as mybir
 
 BF16, F32, U16 = mybir.dt.bfloat16, mybir.dt.float32, mybir.dt.uint16
 SILU = mybir.ActivationFunctionType.Silu
-ADD = mybir.AluOpType.add
 
 P = 128
 ITEMS = 4096
@@ -20,9 +19,8 @@ def tile_denoisedsasrec_kernel(tc, table, pos, w, offs, out):
     nc = tc.nc
     with (
         tc.tile_pool(name="held", bufs=1) as held,
-        tc.tile_pool(name="blocks", bufs=4) as blocks,
-        tc.psum_pool(name="once", bufs=1) as once,
-        tc.psum_pool(name="banks", bufs=4) as banks,
+        tc.tile_pool(name="results", bufs=PIECES * HALVES) as results,
+        tc.psum_pool(name="psum", bufs=1) as psum,
     ):
         offsets = held.tile([P, N // 16], U16, name="offsets")
         weights = held.tile([P, HIDDEN], BF16, name="weights")
@@ -33,38 +31,31 @@ def tile_denoisedsasrec_kernel(tc, table, pos, w, offs, out):
         nc.sync.dma_start(offsets[:], offs)
         nc.sync.dma_start(items[:], table)
 
-        projected_bank = once.tile([P, HALVES, PLACES], F32, name="projected_bank")
-        projected = held.tile([P, HALVES, PLACES], F32, name="projected")
-        for half in range(HALVES):
-            nc.tensor.matmul(
-                projected_bank[:, half, :],
-                weights[:, half * P : (half + 1) * P],
-                places[:],
-                start=True,
-                stop=True,
-            )
-        nc.vector.tensor_copy(projected[:], projected_bank[:])
+        blocks = [(piece, half) for piece in range(PIECES) for half in range(HALVES)]
+        banks = [psum.tile([P, PIECE], F32, name=f"bank{b}") for b in range(len(blocks))]
 
         sequences = PIECE // PLACES
-        for piece in range(PIECES):
+        repeated_places = places[:].unsqueeze(1).to_broadcast([P, sequences, PLACES])
+        for bank, (piece, half) in zip(banks, blocks):
+            nc.tensor.matmul(
+                bank[:].rearrange("p (s l) -> p s l", s=sequences),
+                weights[:, half * P : (half + 1) * P],
+                repeated_places,
+                start=True,
+                stop=False,
+            )
+
+        for bank, (piece, half) in zip(banks, blocks):
             piece_offsets = offsets[:, piece * (PIECE // 16) : (piece + 1) * (PIECE // 16)]
-            for half in range(HALVES):
-                bank = banks.tile([P, PIECE], F32, name="bank")
-                nc.tensor.matmul(
-                    bank[:],
-                    weights[:, half * P : (half + 1) * P],
-                    items[:].indirect(piece_offsets),
-                    start=True,
-                    stop=True,
-                )
-                block = blocks.tile([P, PIECE], F32, name="block")
-                nc.vector.tensor_tensor(
-                    block[:].rearrange("p (s l) -> p s l", s=sequences),
-                    bank[:].rearrange("p (s l) -> p s l", s=sequences),
-                    projected[:, half : half + 1, :].to_broadcast([P, sequences, PLACES]),
-                    ADD,
-                )
-                nc.scalar.activation(block[:], block[:], SILU)
-                nc.sync.dma_start(
-                    out[half * P : (half + 1) * P, piece * PIECE : (piece + 1) * PIECE], block[:]
-                )
+            nc.tensor.matmul(
+                bank[:],
+                weights[:, half * P : (half + 1) * P],
+                items[:].indirect(piece_offsets),
+                start=False,
+                stop=True,
+            )
+            result = results.tile([P, PIECE], F32, name="result")
+            nc.scalar.activation(result[:], bank[:], SILU)
+            nc.sync.dma_start(
+                out[half * P : (half + 1) * P, piece * PIECE : (piece + 1) * PIECE], result[:]
+            )

@@ -11,6 +11,7 @@ N = 2048
 PIECE = 512
 HALVES = HIDDEN // P
 PIECES = N // PIECE
+WARM_UPS = 3
 
 FLOPS = 2 * P * HIDDEN * (N + PLACES)
 
@@ -35,6 +36,17 @@ def tile_denoisedsasrec_kernel(tc, table, pos, w, offs, out):
         banks = [psum.tile([P, PIECE], F32, name=f"bank{b}") for b in range(len(blocks))]
 
         sequences = PIECE // PLACES
+        zeros = held.tile([P, PLACES], BF16, name="zeros")
+        nc.vector.memset(zeros[:], 0.0)
+        for turn in range(WARM_UPS):
+            nc.tensor.matmul(
+                banks[-1][:].rearrange("p (s l) -> p s l", s=sequences),
+                zeros[:],
+                zeros[:].unsqueeze(1).to_broadcast([P, sequences, PLACES]),
+                start=True,
+                stop=True,
+            )
+
         repeated_places = places[:].unsqueeze(1).to_broadcast([P, sequences, PLACES])
         for bank, (piece, half) in zip(banks, blocks):
             nc.tensor.matmul(

@@ -11,7 +11,6 @@ N = 2048
 PIECE = 512
 HALVES = HIDDEN // P
 PIECES = N // PIECE
-WARM_UPS = 3
 
 FLOPS = 2 * P * HIDDEN * (N + PLACES)
 
@@ -30,23 +29,16 @@ def tile_denoisedsasrec_kernel(tc, table, pos, w, offs, out):
         nc.scalar.dma_start(weights[:], w)
         nc.sync.dma_start(places[:], pos)
         nc.sync.dma_start(offsets[:], offs)
-        nc.sync.dma_start(items[:], table)
+        quarter = ITEMS // 4
+        for q in range(4):
+            queue = nc.sync if q % 2 == 0 else nc.scalar
+            columns = slice(q * quarter, (q + 1) * quarter)
+            queue.dma_start(items[:, columns], table[:, columns])
 
         blocks = [(piece, half) for piece in range(PIECES) for half in range(HALVES)]
         banks = [psum.tile([P, PIECE], F32, name=f"bank{b}") for b in range(len(blocks))]
 
         sequences = PIECE // PLACES
-        zeros = held.tile([P, PLACES], BF16, name="zeros")
-        nc.vector.memset(zeros[:], 0.0)
-        for turn in range(WARM_UPS):
-            nc.tensor.matmul(
-                banks[-1][:].rearrange("p (s l) -> p s l", s=sequences),
-                zeros[:],
-                zeros[:].unsqueeze(1).to_broadcast([P, sequences, PLACES]),
-                start=True,
-                stop=True,
-            )
-
         repeated_places = places[:].unsqueeze(1).to_broadcast([P, sequences, PLACES])
         for bank, (piece, half) in zip(banks, blocks):
             nc.tensor.matmul(

@@ -29,11 +29,9 @@ def tile_denoisedsasrec_kernel(tc, table, pos, w, offs, out):
         nc.scalar.dma_start(weights[:], w)
         nc.sync.dma_start(places[:], pos)
         nc.sync.dma_start(offsets[:], offs)
-        quarter = ITEMS // 4
-        for q in range(4):
-            queue = nc.sync if q % 2 == 0 else nc.scalar
-            columns = slice(q * quarter, (q + 1) * quarter)
-            queue.dma_start(items[:, columns], table[:, columns])
+        middle = ITEMS // 2
+        nc.sync.dma_start(items[:, :middle], table[:, :middle])
+        nc.scalar.dma_start(items[:, middle:], table[:, middle:])
 
         blocks = [(piece, half) for piece in range(PIECES) for half in range(HALVES)]
         banks = [psum.tile([P, PIECE], F32, name=f"bank{b}") for b in range(len(blocks))]

@@ -9,8 +9,11 @@ PLACES = 128
 HIDDEN = 256
 N = 2048
 PIECE = 512
-HALVES = HIDDEN // P
 PIECES = N // PIECE
+HALVES = HIDDEN // P
+BLOCKS = PIECES * HALVES
+SEQUENCES = PIECE // PLACES
+TABLE_LOADS = 4
 
 FLOPS = 2 * P * HIDDEN * (N + PLACES)
 
@@ -18,46 +21,52 @@ FLOPS = 2 * P * HIDDEN * (N + PLACES)
 def tile_denoisedsasrec_kernel(tc, table, pos, w, offs, out):
     nc = tc.nc
     with (
-        tc.tile_pool(name="held", bufs=1) as held,
-        tc.tile_pool(name="results", bufs=PIECES * HALVES) as results,
+        tc.tile_pool(name="inputs", bufs=1) as inputs,
+        tc.tile_pool(name="results", bufs=BLOCKS) as results,
         tc.psum_pool(name="psum", bufs=1) as psum,
     ):
-        offsets = held.tile([P, N // 16], U16, name="offsets")
-        weights = held.tile([P, HIDDEN], BF16, name="weights")
-        places = held.tile([P, PLACES], BF16, name="places")
-        items = held.tile([P, ITEMS], BF16, name="items")
-        nc.scalar.dma_start(weights[:], w)
-        nc.sync.dma_start(places[:], pos)
+        w_tile = inputs.tile([P, HIDDEN], BF16, name="w_tile")
+        pos_tile = inputs.tile([P, PLACES], BF16, name="pos_tile")
+        offsets = inputs.tile([P, N // 16], U16, name="offsets")
+        table_tile = inputs.tile([P, ITEMS], BF16, name="table_tile")
+
+        nc.scalar.dma_start(w_tile[:], w)
+        nc.sync.dma_start(pos_tile[:], pos)
         nc.sync.dma_start(offsets[:], offs)
-        middle = ITEMS // 2
-        nc.sync.dma_start(items[:, :middle], table[:, :middle])
-        nc.scalar.dma_start(items[:, middle:], table[:, middle:])
+        width = ITEMS // TABLE_LOADS
+        for load in range(TABLE_LOADS):
+            queue = nc.sync if load % 2 == 0 else nc.scalar
+            columns = slice(load * width, (load + 1) * width)
+            queue.dma_start(table_tile[:, columns], table[:, columns])
 
-        blocks = [(piece, half) for piece in range(PIECES) for half in range(HALVES)]
-        banks = [psum.tile([P, PIECE], F32, name=f"bank{b}") for b in range(len(blocks))]
+        banks = [
+            [psum.tile([P, PIECE], F32, name=f"bank_{piece}_{half}") for half in range(HALVES)]
+            for piece in range(PIECES)
+        ]
 
-        sequences = PIECE // PLACES
-        repeated_places = places[:].unsqueeze(1).to_broadcast([P, sequences, PLACES])
-        for bank, (piece, half) in zip(banks, blocks):
-            nc.tensor.matmul(
-                bank[:].rearrange("p (s l) -> p s l", s=sequences),
-                weights[:, half * P : (half + 1) * P],
-                repeated_places,
-                start=True,
-                stop=False,
-            )
+        repeated_pos = pos_tile[:].unsqueeze(1).to_broadcast([P, SEQUENCES, PLACES])
+        for piece in range(PIECES):
+            for half in range(HALVES):
+                nc.tensor.matmul(
+                    banks[piece][half][:].rearrange("p (s l) -> p s l", s=SEQUENCES),
+                    w_tile[:, half * P : (half + 1) * P],
+                    repeated_pos,
+                    start=True,
+                    stop=False,
+                )
 
-        for bank, (piece, half) in zip(banks, blocks):
+        for piece in range(PIECES):
             piece_offsets = offsets[:, piece * (PIECE // 16) : (piece + 1) * (PIECE // 16)]
-            nc.tensor.matmul(
-                bank[:],
-                weights[:, half * P : (half + 1) * P],
-                items[:].indirect(piece_offsets),
-                start=False,
-                stop=True,
-            )
-            result = results.tile([P, PIECE], F32, name="result")
-            nc.scalar.activation(result[:], bank[:], SILU)
-            nc.sync.dma_start(
-                out[half * P : (half + 1) * P, piece * PIECE : (piece + 1) * PIECE], result[:]
-            )
+            for half in range(HALVES):
+                nc.tensor.matmul(
+                    banks[piece][half][:],
+                    w_tile[:, half * P : (half + 1) * P],
+                    table_tile[:].indirect(piece_offsets),
+                    start=False,
+                    stop=True,
+                )
+                result = results.tile([P, PIECE], F32, name="result")
+                nc.scalar.activation(result[:], banks[piece][half][:], SILU)
+                nc.sync.dma_start(
+                    out[half * P : (half + 1) * P, piece * PIECE : (piece + 1) * PIECE], result[:]
+                )

@@ -11,9 +11,10 @@ N = 2048
 PIECE = 512
 PIECES = N // PIECE
 HALVES = HIDDEN // P
-BLOCKS = PIECES * HALVES
 SEQUENCES = PIECE // PLACES
 TABLE_LOADS = 4
+BLOCKS = [(piece, half) for piece in range(PIECES) for half in range(HALVES)]
+POS_LAST = 1
 
 FLOPS = 2 * P * HIDDEN * (N + PLACES)
 
@@ -22,7 +23,7 @@ def tile_denoisedsasrec_kernel(tc, table, pos, w, offs, out):
     nc = tc.nc
     with (
         tc.tile_pool(name="inputs", bufs=1) as inputs,
-        tc.tile_pool(name="results", bufs=BLOCKS) as results,
+        tc.tile_pool(name="results", bufs=len(BLOCKS)) as results,
         tc.psum_pool(name="psum", bufs=1) as psum,
     ):
         w_tile = inputs.tile([P, HIDDEN], BF16, name="w_tile")
@@ -33,40 +34,55 @@ def tile_denoisedsasrec_kernel(tc, table, pos, w, offs, out):
         nc.scalar.dma_start(w_tile[:], w)
         nc.sync.dma_start(pos_tile[:], pos)
         nc.sync.dma_start(offsets[:], offs)
-        width = ITEMS // TABLE_LOADS
+        load_width = ITEMS // TABLE_LOADS
         for load in range(TABLE_LOADS):
             queue = nc.sync if load % 2 == 0 else nc.scalar
-            columns = slice(load * width, (load + 1) * width)
+            columns = slice(load * load_width, (load + 1) * load_width)
             queue.dma_start(table_tile[:, columns], table[:, columns])
 
-        banks = [
-            [psum.tile([P, PIECE], F32, name=f"bank_{piece}_{half}") for half in range(HALVES)]
-            for piece in range(PIECES)
-        ]
+        banks = {
+            block: psum.tile([P, PIECE], F32, name=f"bank_{block[0]}_{block[1]}")
+            for block in BLOCKS
+        }
 
-        repeated_pos = pos_tile[:].unsqueeze(1).to_broadcast([P, SEQUENCES, PLACES])
-        for piece in range(PIECES):
-            for half in range(HALVES):
-                nc.tensor.matmul(
-                    banks[piece][half][:].rearrange("p (s l) -> p s l", s=SEQUENCES),
-                    w_tile[:, half * P : (half + 1) * P],
-                    repeated_pos,
-                    start=True,
-                    stop=False,
-                )
+        def add_pos(block, first):
+            half = block[1]
+            nc.tensor.matmul(
+                banks[block][:].rearrange("p (s l) -> p s l", s=SEQUENCES),
+                w_tile[:, half * P : (half + 1) * P],
+                pos_tile[:].unsqueeze(1).to_broadcast([P, SEQUENCES, PLACES]),
+                start=first,
+                stop=not first,
+            )
 
-        for piece in range(PIECES):
+        def add_looked_up(block, first):
+            piece, half = block
             piece_offsets = offsets[:, piece * (PIECE // 16) : (piece + 1) * (PIECE // 16)]
-            for half in range(HALVES):
-                nc.tensor.matmul(
-                    banks[piece][half][:],
-                    w_tile[:, half * P : (half + 1) * P],
-                    table_tile[:].indirect(piece_offsets),
-                    start=False,
-                    stop=True,
-                )
-                result = results.tile([P, PIECE], F32, name="result")
-                nc.scalar.activation(result[:], banks[piece][half][:], SILU)
-                nc.sync.dma_start(
-                    out[half * P : (half + 1) * P, piece * PIECE : (piece + 1) * PIECE], result[:]
-                )
+            nc.tensor.matmul(
+                banks[block][:],
+                w_tile[:, half * P : (half + 1) * P],
+                table_tile[:].indirect(piece_offsets),
+                start=first,
+                stop=not first,
+            )
+
+        def finish(block):
+            piece, half = block
+            result = results.tile([P, PIECE], F32, name="result")
+            nc.scalar.activation(result[:], banks[block][:], SILU)
+            nc.sync.dma_start(
+                out[half * P : (half + 1) * P, piece * PIECE : (piece + 1) * PIECE], result[:]
+            )
+
+        pos_first = BLOCKS[: len(BLOCKS) - POS_LAST]
+        pos_last = BLOCKS[len(BLOCKS) - POS_LAST :]
+        for block in pos_first:
+            add_pos(block, first=True)
+        for block in pos_first:
+            add_looked_up(block, first=False)
+            finish(block)
+        for block in pos_last:
+            add_looked_up(block, first=True)
+        for block in pos_last:
+            add_pos(block, first=False)
+            finish(block)

@@ -70,7 +70,8 @@ def tile_denoisedsasrec_kernel(tc, table, pos, w, offs, out):
             piece, half = block
             result = results.tile([P, PIECE], F32, name="result")
             nc.scalar.activation(result[:], banks[block][:], SILU)
-            nc.sync.dma_start(
+            queue = nc.sync if half == 0 else nc.scalar
+            queue.dma_start(
                 out[half * P : (half + 1) * P, piece * PIECE : (piece + 1) * PIECE], result[:]
             )
 

@@ -14,7 +14,8 @@ HALVES = HIDDEN // P
 SEQUENCES = PIECE // PLACES
 TABLE_LOADS = 4
 BLOCKS = [(piece, half) for piece in range(PIECES) for half in range(HALVES)]
-POS_LAST = 1
+*POS_FIRST, POS_BY_VECTOR, POS_LAST = BLOCKS
+VECTOR_PARTS = 2
 
 FLOPS = 2 * P * HIDDEN * (N + PLACES)
 
@@ -55,7 +56,7 @@ def tile_denoisedsasrec_kernel(tc, table, pos, w, offs, out):
                 stop=not first,
             )
 
-        def add_looked_up(block, first):
+        def add_looked_up(block, first, last):
             piece, half = block
             piece_offsets = offsets[:, piece * (PIECE // 16) : (piece + 1) * (PIECE // 16)]
             nc.tensor.matmul(
@@ -63,27 +64,49 @@ def tile_denoisedsasrec_kernel(tc, table, pos, w, offs, out):
                 w_tile[:, half * P : (half + 1) * P],
                 table_tile[:].indirect(piece_offsets),
                 start=first,
-                stop=not first,
+                stop=last,
             )
 
-        def finish(block):
+        def store(block, result):
             piece, half = block
-            result = results.tile([P, PIECE], F32, name="result")
-            nc.scalar.activation(result[:], banks[block][:], SILU)
             queue = nc.sync if half == 0 else nc.scalar
             queue.dma_start(
                 out[half * P : (half + 1) * P, piece * PIECE : (piece + 1) * PIECE], result[:]
             )
 
-        pos_first = BLOCKS[: len(BLOCKS) - POS_LAST]
-        pos_last = BLOCKS[len(BLOCKS) - POS_LAST :]
-        for block in pos_first:
+        def finish(block):
+            result = results.tile([P, PIECE], F32, name="result")
+            nc.scalar.activation(result[:], banks[block][:], SILU)
+            store(block, result)
+
+        for block in POS_FIRST:
             add_pos(block, first=True)
-        for block in pos_first:
-            add_looked_up(block, first=False)
+        half = POS_BY_VECTOR[1]
+        pos_product = inputs.tile([P, PLACES], F32, name="pos_product")
+        nc.tensor.matmul(
+            banks[POS_LAST][:, :PLACES], w_tile[:, half * P : (half + 1) * P], pos_tile[:]
+        )
+        nc.vector.tensor_copy(pos_product[:], banks[POS_LAST][:, :PLACES])
+
+        for block in POS_FIRST:
+            add_looked_up(block, first=False, last=True)
             finish(block)
-        for block in pos_last:
-            add_looked_up(block, first=True)
-        for block in pos_last:
-            add_pos(block, first=False)
-            finish(block)
+
+        add_looked_up(POS_BY_VECTOR, first=True, last=True)
+        sums = inputs.tile([P, PIECE], F32, name="sums")
+        result = results.tile([P, PIECE], F32, name="result")
+        width = PIECE // VECTOR_PARTS
+        for part in range(VECTOR_PARTS):
+            columns = slice(part * width, (part + 1) * width)
+            nc.vector.tensor_tensor(
+                sums[:, columns].rearrange("p (s l) -> p s l", l=PLACES),
+                banks[POS_BY_VECTOR][:, columns].rearrange("p (s l) -> p s l", l=PLACES),
+                pos_product[:].unsqueeze(1).to_broadcast([P, width // PLACES, PLACES]),
+                mybir.AluOpType.add,
+            )
+            nc.scalar.activation(result[:, columns], sums[:, columns], SILU)
+        store(POS_BY_VECTOR, result)
+
+        add_looked_up(POS_LAST, first=True, last=False)
+        add_pos(POS_LAST, first=False)
+        finish(POS_LAST)

@@ -14,8 +14,8 @@ HALVES = HIDDEN // P
 SEQUENCES = PIECE // PLACES
 TABLE_LOADS = 4
 BLOCKS = [(piece, half) for piece in range(PIECES) for half in range(HALVES)]
-*POS_FIRST, POS_BY_VECTOR, POS_LAST = BLOCKS
-VECTOR_PARTS = 2
+POS_BY_VECTOR, *POS_FIRST, POS_LAST = BLOCKS
+VECTOR_LOOK_UPS = 2
 
 FLOPS = 2 * P * HIDDEN * (N + PLACES)
 
@@ -56,11 +56,11 @@ def tile_denoisedsasrec_kernel(tc, table, pos, w, offs, out):
                 stop=not first,
             )
 
-        def add_looked_up(block, first, last):
-            piece, half = block
-            piece_offsets = offsets[:, piece * (PIECE // 16) : (piece + 1) * (PIECE // 16)]
+        def look_up(target, half, entry, first, last):
+            entries = target.shape[1]
+            piece_offsets = offsets[:, entry // 16 : (entry + entries) // 16]
             nc.tensor.matmul(
-                banks[block][:],
+                target,
                 w_tile[:, half * P : (half + 1) * P],
                 table_tile[:].indirect(piece_offsets),
                 start=first,
@@ -79,34 +79,31 @@ def tile_denoisedsasrec_kernel(tc, table, pos, w, offs, out):
             nc.scalar.activation(result[:], banks[block][:], SILU)
             store(block, result)
 
+        piece, half = POS_BY_VECTOR
+        product_bank = banks[POS_BY_VECTOR][:, :PLACES]
+        nc.tensor.matmul(product_bank, w_tile[:, half * P : (half + 1) * P], pos_tile[:])
+        pos_product = inputs.tile([P, PLACES], F32, name="pos_product")
+        nc.vector.tensor_copy(pos_product[:], product_bank)
         for block in POS_FIRST:
             add_pos(block, first=True)
-        half = POS_BY_VECTOR[1]
-        pos_product = inputs.tile([P, PLACES], F32, name="pos_product")
-        nc.tensor.matmul(
-            banks[POS_LAST][:, :PLACES], w_tile[:, half * P : (half + 1) * P], pos_tile[:]
-        )
-        nc.vector.tensor_copy(pos_product[:], banks[POS_LAST][:, :PLACES])
 
-        for block in POS_FIRST:
-            add_looked_up(block, first=False, last=True)
-            finish(block)
-
-        add_looked_up(POS_BY_VECTOR, first=True, last=True)
-        sums = inputs.tile([P, PIECE], F32, name="sums")
         result = results.tile([P, PIECE], F32, name="result")
-        width = PIECE // VECTOR_PARTS
-        for part in range(VECTOR_PARTS):
-            columns = slice(part * width, (part + 1) * width)
-            nc.vector.tensor_tensor(
-                sums[:, columns].rearrange("p (s l) -> p s l", l=PLACES),
-                banks[POS_BY_VECTOR][:, columns].rearrange("p (s l) -> p s l", l=PLACES),
-                pos_product[:].unsqueeze(1).to_broadcast([P, width // PLACES, PLACES]),
-                mybir.AluOpType.add,
-            )
-            nc.scalar.activation(result[:, columns], sums[:, columns], SILU)
+        width = PIECE // VECTOR_LOOK_UPS
+        vector_banks = (banks[POS_BY_VECTOR], banks[POS_LAST])
+        for part, bank in enumerate(vector_banks):
+            look_up(bank[:, :width], half, piece * PIECE + part * width, first=True, last=True)
+        for sequence in range(SEQUENCES):
+            part, start = divmod(sequence * PLACES, width)
+            looked_up_sum = vector_banks[part][:, start : start + PLACES]
+            total = inputs.tile([P, PLACES], F32, name=f"total_{sequence}")
+            nc.vector.tensor_tensor(total[:], looked_up_sum, pos_product[:], mybir.AluOpType.add)
+            columns = slice(sequence * PLACES, (sequence + 1) * PLACES)
+            nc.scalar.activation(result[:, columns], total[:], SILU)
         store(POS_BY_VECTOR, result)
 
-        add_looked_up(POS_LAST, first=True, last=False)
+        for block in POS_FIRST:
+            look_up(banks[block][:], block[1], block[0] * PIECE, first=False, last=True)
+            finish(block)
+        look_up(banks[POS_LAST][:], POS_LAST[1], POS_LAST[0] * PIECE, first=True, last=False)
         add_pos(POS_LAST, first=False)
         finish(POS_LAST)

@@ -14,7 +14,9 @@ HALVES = HIDDEN // P
 SEQUENCES = PIECE // PLACES
 TABLE_LOADS = 4
 BLOCKS = [(piece, half) for piece in range(PIECES) for half in range(HALVES)]
-POS_BY_VECTOR, *POS_FIRST, POS_LAST = BLOCKS
+POS_BY_VECTOR = BLOCKS[len(BLOCKS) // 2]
+POS_LAST = BLOCKS[-1]
+POS_FIRST = [block for block in BLOCKS if block not in (POS_BY_VECTOR, POS_LAST)]
 VECTOR_LOOK_UPS = 2
 
 FLOPS = 2 * P * HIDDEN * (N + PLACES)
@@ -79,7 +81,7 @@ def tile_denoisedsasrec_kernel(tc, table, pos, w, offs, out):
             nc.scalar.activation(result[:], banks[block][:], SILU)
             store(block, result)
 
-        piece, half = POS_BY_VECTOR
+        half = POS_BY_VECTOR[1]
         product_bank = banks[POS_BY_VECTOR][:, :PLACES]
         nc.tensor.matmul(product_bank, w_tile[:, half * P : (half + 1) * P], pos_tile[:])
         pos_product = inputs.tile([P, PLACES], F32, name="pos_product")
@@ -87,23 +89,31 @@ def tile_denoisedsasrec_kernel(tc, table, pos, w, offs, out):
         for block in POS_FIRST:
             add_pos(block, first=True)
 
-        result = results.tile([P, PIECE], F32, name="result")
-        width = PIECE // VECTOR_LOOK_UPS
-        vector_banks = (banks[POS_BY_VECTOR], banks[POS_LAST])
-        for part, bank in enumerate(vector_banks):
-            look_up(bank[:, :width], half, piece * PIECE + part * width, first=True, last=True)
-        for sequence in range(SEQUENCES):
-            part, start = divmod(sequence * PLACES, width)
-            looked_up_sum = vector_banks[part][:, start : start + PLACES]
-            total = inputs.tile([P, PLACES], F32, name=f"total_{sequence}")
-            nc.vector.tensor_tensor(total[:], looked_up_sum, pos_product[:], mybir.AluOpType.add)
-            columns = slice(sequence * PLACES, (sequence + 1) * PLACES)
-            nc.scalar.activation(result[:, columns], total[:], SILU)
-        store(POS_BY_VECTOR, result)
+        def finish_by_vector(block):
+            piece, half = block
+            result = results.tile([P, PIECE], F32, name="result")
+            width = PIECE // VECTOR_LOOK_UPS
+            vector_banks = (banks[block], banks[POS_LAST])
+            for part, bank in enumerate(vector_banks):
+                look_up(bank[:, :width], half, piece * PIECE + part * width, first=True, last=True)
+            for sequence in range(SEQUENCES):
+                part, start = divmod(sequence * PLACES, width)
+                looked_up_sum = vector_banks[part][:, start : start + PLACES]
+                total = inputs.tile([P, PLACES], F32, name=f"total_{sequence}")
+                nc.vector.tensor_tensor(
+                    total[:], looked_up_sum, pos_product[:], mybir.AluOpType.add
+                )
+                columns = slice(sequence * PLACES, (sequence + 1) * PLACES)
+                nc.scalar.activation(result[:, columns], total[:], SILU)
+            store(block, result)
 
-        for block in POS_FIRST:
-            look_up(banks[block][:], block[1], block[0] * PIECE, first=False, last=True)
+        for block in BLOCKS:
+            piece, half = block
+            if block == POS_BY_VECTOR:
+                finish_by_vector(block)
+                continue
+            late = block == POS_LAST
+            look_up(banks[block][:], half, piece * PIECE, first=late, last=not late)
+            if late:
+                add_pos(block, first=False)
             finish(block)
-        look_up(banks[POS_LAST][:], POS_LAST[1], POS_LAST[0] * PIECE, first=True, last=False)
-        add_pos(POS_LAST, first=False)
-        finish(POS_LAST)

@@ -93,17 +93,16 @@ def tile_denoisedsasrec_kernel(tc, table, pos, w, offs, out):
             piece, half = block
             result = results.tile([P, PIECE], F32, name="result")
             width = PIECE // VECTOR_LOOK_UPS
-            vector_banks = (banks[block], banks[POS_LAST])
-            for part, bank in enumerate(vector_banks):
+            for part, bank in enumerate((banks[block], banks[POS_LAST])):
                 look_up(bank[:, :width], half, piece * PIECE + part * width, first=True, last=True)
-            for sequence in range(SEQUENCES):
-                part, start = divmod(sequence * PLACES, width)
-                looked_up_sum = vector_banks[part][:, start : start + PLACES]
-                total = inputs.tile([P, PLACES], F32, name=f"total_{sequence}")
+                total = inputs.tile([P, width], F32, name=f"total_{part}")
                 nc.vector.tensor_tensor(
-                    total[:], looked_up_sum, pos_product[:], mybir.AluOpType.add
+                    total[:].rearrange("p (s l) -> p s l", l=PLACES),
+                    bank[:, :width].rearrange("p (s l) -> p s l", l=PLACES),
+                    pos_product[:].unsqueeze(1).to_broadcast([P, width // PLACES, PLACES]),
+                    mybir.AluOpType.add,
                 )
-                columns = slice(sequence * PLACES, (sequence + 1) * PLACES)
+                columns = slice(part * width, (part + 1) * width)
                 nc.scalar.activation(result[:, columns], total[:], SILU)
             store(block, result)
 

@@ -71,8 +71,7 @@ def tile_denoisedsasrec_kernel(tc, table, pos, w, offs, out):
 
         def store(block, result):
             piece, half = block
-            queue = nc.sync if half == 0 else nc.scalar
-            queue.dma_start(
+            nc.sync.dma_start(
                 out[half * P : (half + 1) * P, piece * PIECE : (piece + 1) * PIECE], result[:]
             )
 

import concourse.mybir as mybir

BF16, F32, U16 = mybir.dt.bfloat16, mybir.dt.float32, mybir.dt.uint16
SILU = mybir.ActivationFunctionType.Silu

P = 128
ITEMS = 4096
PLACES = 128
HIDDEN = 256
N = 2048
PIECE = 512
PIECES = N // PIECE
HALVES = HIDDEN // P
SEQUENCES = PIECE // PLACES
TABLE_LOADS = 4
BLOCKS = [(piece, half) for piece in range(PIECES) for half in range(HALVES)]
POS_BY_VECTOR = BLOCKS[len(BLOCKS) // 2]
POS_LAST = BLOCKS[-1]
POS_FIRST = [block for block in BLOCKS if block not in (POS_BY_VECTOR, POS_LAST)]
VECTOR_LOOK_UPS = 2

FLOPS = 2 * P * HIDDEN * (N + PLACES)


def tile_denoisedsasrec_kernel(tc, table, pos, w, offs, out):
    nc = tc.nc
    with (
        tc.tile_pool(name="inputs", bufs=1) as inputs,
        tc.tile_pool(name="results", bufs=len(BLOCKS)) as results,
        tc.psum_pool(name="psum", bufs=1) as psum,
    ):
        w_tile = inputs.tile([P, HIDDEN], BF16, name="w_tile")
        pos_tile = inputs.tile([P, PLACES], BF16, name="pos_tile")
        offsets = inputs.tile([P, N // 16], U16, name="offsets")
        table_tile = inputs.tile([P, ITEMS], BF16, name="table_tile")

        nc.scalar.dma_start(w_tile[:], w)
        nc.sync.dma_start(pos_tile[:], pos)
        nc.sync.dma_start(offsets[:], offs)
        load_width = ITEMS // TABLE_LOADS
        for load in range(TABLE_LOADS):
            queue = nc.sync if load % 2 == 0 else nc.scalar
            columns = slice(load * load_width, (load + 1) * load_width)
            queue.dma_start(table_tile[:, columns], table[:, columns])

        banks = {
            block: psum.tile([P, PIECE], F32, name=f"bank_{block[0]}_{block[1]}")
            for block in BLOCKS
        }

        def add_pos(block, first):
            half = block[1]
            nc.tensor.matmul(
                banks[block][:].rearrange("p (s l) -> p s l", s=SEQUENCES),
                w_tile[:, half * P : (half + 1) * P],
                pos_tile[:].unsqueeze(1).to_broadcast([P, SEQUENCES, PLACES]),
                start=first,
                stop=not first,
            )

        def look_up(target, half, entry, first, last):
            entries = target.shape[1]
            piece_offsets = offsets[:, entry // 16 : (entry + entries) // 16]
            nc.tensor.matmul(
                target,
                w_tile[:, half * P : (half + 1) * P],
                table_tile[:].indirect(piece_offsets),
                start=first,
                stop=last,
            )

        def store(block, result):
            piece, half = block
            nc.sync.dma_start(
                out[half * P : (half + 1) * P, piece * PIECE : (piece + 1) * PIECE], result[:]
            )

        def finish(block):
            result = results.tile([P, PIECE], F32, name="result")
            nc.scalar.activation(result[:], banks[block][:], SILU)
            store(block, result)

        half = POS_BY_VECTOR[1]
        product_bank = banks[POS_BY_VECTOR][:, :PLACES]
        nc.tensor.matmul(product_bank, w_tile[:, half * P : (half + 1) * P], pos_tile[:])
        pos_product = inputs.tile([P, PLACES], F32, name="pos_product")
        nc.vector.tensor_copy(pos_product[:], product_bank)
        for block in POS_FIRST:
            add_pos(block, first=True)

        def finish_by_vector(block):
            piece, half = block
            result = results.tile([P, PIECE], F32, name="result")
            width = PIECE // VECTOR_LOOK_UPS
            for part, bank in enumerate((banks[block], banks[POS_LAST])):
                look_up(bank[:, :width], half, piece * PIECE + part * width, first=True, last=True)
                total = inputs.tile([P, width], F32, name=f"total_{part}")
                nc.vector.tensor_tensor(
                    total[:].rearrange("p (s l) -> p s l", l=PLACES),
                    bank[:, :width].rearrange("p (s l) -> p s l", l=PLACES),
                    pos_product[:].unsqueeze(1).to_broadcast([P, width // PLACES, PLACES]),
                    mybir.AluOpType.add,
                )
                columns = slice(part * width, (part + 1) * width)
                nc.scalar.activation(result[:, columns], total[:], SILU)
            store(block, result)

        for block in BLOCKS:
            piece, half = block
            if block == POS_BY_VECTOR:
                finish_by_vector(block)
                continue
            late = block == POS_LAST
            look_up(banks[block][:], half, piece * PIECE, first=late, last=not late)
            if late:
                add_pos(block, first=False)
            finish(block)
